import numpy as np
import ml_dtypes


def mxq(x, axis, fmt="e4m3"):
    dtype, down = {"e4m3": (ml_dtypes.float8_e4m3fn, 7), "e5m2": (ml_dtypes.float8_e5m2, 14)}[fmt]
    v = np.moveaxis(np.asarray(x, np.float32).astype(ml_dtypes.bfloat16).astype(np.float64), axis, -1)
    blocks = v.reshape(v.shape[:-1] + (-1, 32))
    amax = np.abs(blocks).max(-1, keepdims=True)
    byte = np.maximum(np.where(amax > 0, np.frexp(amax)[1] - 1 + 127, 0) - down, 1)
    scale = np.exp2(byte - 127.0)
    codes = (blocks / scale).astype(np.float32).astype(dtype).astype(np.float64)
    return np.moveaxis((codes * scale).reshape(v.shape), -1, axis)


WIDE = False


def mx_kscale(k):
    if not WIDE:
        return np.ones(k)
    levels = np.array([10, -10, 5, -5, 0])
    if k % 512:
        return np.exp2(np.random.permutation(np.resize(levels, k // 32))).repeat(32)
    a = np.empty((k // 512, 16))
    for p in range(k // 512):
        a[p, :8] = np.random.permutation(np.resize(levels, 8))
        for g in range(8):
            far = levels[np.abs(levels - a[p, g]) >= 10]
            a[p, g + 8] = far[np.random.randint(len(far))]
    return np.exp2(a.ravel()).repeat(32)


BF16 = ml_dtypes.bfloat16


def bf(x):
    return np.asarray(x, np.float32).astype(BF16)


def f64(x):
    return np.asarray(x).astype(np.float64)


B, S, D, E = 2, 1024, 1024, 1024


def draw0():
    s, t = mx_kscale(S), mx_kscale(D)
    return {"q": bf(np.random.standard_normal((B, S, D)) / t),
            "k": bf(np.random.standard_normal((B, S, D)) * s[:, None] * t),
            "v": bf(np.random.standard_normal((B, S, E)) / s[:, None])}


def core(q, k, v):
    scale = 1.0 / np.sqrt(q.shape[1])
    qn = f64(q) * scale
    kn = f64(k) * scale
    kv_mat = mxq(kn, 1, "e4m3").transpose(0, 2, 1) @ mxq(f64(v), 1, "e4m3")
    out = mxq(qn, 2, "e4m3") @ mxq(kv_mat, 1, "e4m3")
    return out


def e4m3fn_bytes(y):
    return np.clip(np.asarray(y, np.float64), -448.0, 448.0).astype(np.float32).astype(ml_dtypes.float8_e4m3fn).view(np.uint8)


def e4m3fn_values(b):
    return np.asarray(b, np.uint8).view(ml_dtypes.float8_e4m3fn).astype(np.float64)


def setup_inputs():
    d = draw0()
    x0 = np.asarray(d['v']).astype(np.float64)
    s = (np.max(np.abs(x0), axis=(0, 2), keepdims=True) / 448.0).astype(np.float32)
    out = {}
    for k, v in d.items():
        if k == 'v':
            out['v_bytes'] = e4m3fn_bytes(x0 / s.astype(np.float64))
            out['v_scale'] = s
        else:
            out[k] = v
    return out


def reference(q, k, v_bytes, v_scale):
    return core(q, k, e4m3fn_values(v_bytes) * v_scale.astype(np.float64))

@@ -1,0 +1,219 @@
+from contextlib import ExitStack
+
+import concourse.mybir as mybir
+from concourse.masks import make_identity
+
+B, S, D, E = 2, 1024, 1024, 1024
+FLOPS = 2 * B * (D * S * E + S * D * E)
+
+F32 = mybir.dt.float32
+BF16 = mybir.dt.bfloat16
+U32 = mybir.dt.uint32
+U8 = mybir.dt.uint8
+FP8 = mybir.dt.float8_e4m3fn
+FP8X4 = mybir.dt.float8_e4m3fn_x4
+COPY = mybir.ActivationFunctionType.Copy
+MULT = mybir.AluOpType.mult
+
+P = 128
+PACK = 4
+HALF = 512
+INV = 1.0 / 32.0
+
+
+def tile_efficientattention_kernel(tc, q, k, v_bytes, v_scale, out):
+    nc = tc.nc
+    with ExitStack() as ctx:
+        keep = ctx.enter_context(tc.tile_pool(name="keep", bufs=1))
+        raw = ctx.enter_context(tc.tile_pool(name="raw", bufs=4))
+        work = ctx.enter_context(tc.tile_pool(name="work", bufs=3))
+        psum = ctx.enter_context(tc.psum_pool(name="psum", bufs=8))
+        ctx.enter_context(tc.manual_schedule())
+
+        scl = keep.tile([P, 2, PACK], F32, name="scl")
+        nc.scalar.dma_start(out=scl[:], in_=v_scale.rearrange("o (g p j) x -> p (o g) (j x)", p=P, j=PACK))
+        ident = keep.tile([P, P], F32, name="ident")
+        make_identity(nc, ident[:])
+        warm = keep.tile([P, 1], F32, name="warm")
+        nc.vector.memset(warm[:], 0.0)
+        nc.scalar.activation(out=warm[:], in_=warm[:], func=COPY, scale=1.0)
+
+        kc = [keep.tile([P, 2, D], U32, name=f"kc{b}", align_bytes=64) for b in range(B)]
+        ks = [keep.tile([P, 2, D], U8, name=f"ks{b}", align_bytes=64) for b in range(B)]
+        vc = [keep.tile([P, 2, E], U32, name=f"vc{b}", align_bytes=64) for b in range(B)]
+        vs = [keep.tile([P, 2, E], U8, name=f"vs{b}", align_bytes=64) for b in range(B)]
+        qc = [keep.tile([P, 2, S], U32, name=f"qc{b}", align_bytes=64) for b in range(B)]
+        qs = [keep.tile([P, 2, S], U8, name=f"qs{b}", align_bytes=64) for b in range(B)]
+        mc = [keep.tile([P, 2, E], U32, name=f"mc{b}", align_bytes=64) for b in range(B)]
+        ms = [keep.tile([P, 2, E], U8, name=f"ms{b}", align_bytes=64) for b in range(B)]
+
+        k_raw, v_raw, q_raw = {}, {}, {}
+        v_wide, k_grp, v_grp, q_grp, m_grp, xt, acc, res = {}, {}, {}, {}, {}, {}, {}, {}
+
+        def load_k(b, G, g):
+            t = raw.tile([P, PACK, HALF], BF16, name="k_raw", bufs=5)
+            nc.sync.dma_start(out=t[:], in_=k[b].rearrange("(g p j) d -> g p j d", p=P, j=PACK)[g][:, :, G * HALF:(G + 1) * HALF])
+            k_raw[b, G, g] = t
+
+        def load_v(b, g):
+            t = raw.tile([P, PACK, E], U8, name="v_raw", bufs=2)
+            nc.sync.dma_start(out=t[:], in_=v_bytes[b].rearrange("(g p j) e -> g p j e", p=P, j=PACK)[g])
+            v_raw[b, g] = t
+
+        def load_q(b, a):
+            t = raw.tile([P, 4, D], BF16, name="q_raw", bufs=4)
+            nc.sync.dma_start(out=t[:], in_=q[b].rearrange("(p r) d -> p r d", r=8)[:, 4 * a:4 * a + 4, :])
+            q_raw[b, a] = t
+
+        def k_interleave(b, G, g):
+            t = work.tile([P, HALF * PACK], BF16, name="k_grp", align_bytes=64, bufs=2)
+            nc.vector.tensor_scalar(
+                out=t[:].rearrange("p (t m j) -> p t m j", t=PACK, j=PACK),
+                in0=k_raw[b, G, g][:].rearrange("p j (m t) -> p t m j", t=PACK),
+                scalar1=INV, scalar2=None, op0=MULT)
+            k_grp[b, G, g] = t
+
+        def k_quant(b, G, g):
+            c = slice(G * HALF, (G + 1) * HALF)
+            nc.vector.quantize_mx(out=kc[b][:, g, c].bitcast(FP8X4), scales=ks[b][:, g, c], in_=k_grp[b, G, g][:])
+
+        def v_widen(b, h, g, eng):
+            t = work.tile([P, PACK, HALF], BF16, name="v_wide", bufs=3)
+            for j in range(PACK):
+                src = v_raw[b, g][:, j, h * HALF:(h + 1) * HALF].bitcast(FP8)
+                if eng == "S":
+                    nc.scalar.activation(out=t[:, j, :], in_=src, func=COPY, scale=scl[:, g, j:j + 1])
+                else:
+                    nc.vector.tensor_scalar(out=t[:, j, :], in0=src, scalar1=scl[:, g, j:j + 1], scalar2=None, op0=MULT)
+            v_wide[b, h, g] = t
+
+        def v_interleave(b, h, g):
+            t = work.tile([P, HALF * PACK], BF16, name="v_grp", align_bytes=64)
+            nc.vector.tensor_copy(out=t[:].rearrange("p (e j) -> p e j", j=PACK), in_=v_wide[b, h, g][:].rearrange("p j e -> p e j"))
+            v_grp[b, h, g] = t
+
+        def v_quant(b, h, g):
+            c = slice(h * HALF, (h + 1) * HALF)
+            nc.vector.quantize_mx(out=vc[b][:, g, c].bitcast(FP8X4), scales=vs[b][:, g, c], in_=v_grp[b, h, g][:])
+
+        def q_transpose(b, G, i):
+            x = psum.tile([P, 2, 2, P], F32, name="bank")
+            for r in range(2):
+                row = 2 * i + r
+                words = q_raw[b, row // 4][:, row % 4, :].bitcast(F32)
+                for u in range(2):
+                    nc.tensor.transpose(x[:, r, u, :], words[:, 256 * G + u:256 * (G + 1):2], ident[:])
+            xt[b, G, i] = x
+
+        def q_copy(b, G, i, eng):
+            if i == 0:
+                q_grp[b, G] = work.tile([P, S * PACK], BF16, name="q_grp", align_bytes=64, bufs=4)
+            dst = q_grp[b, G][:, i * 1024:(i + 1) * 1024].bitcast(F32).rearrange("p (r n u) -> p r n u", r=2, u=2)
+            src = xt[b, G, i][:].rearrange("p r u n -> p r n u")
+            if eng == "S":
+                nc.scalar.copy(out=dst, in_=src)
+            else:
+                nc.vector.tensor_copy(out=dst, in_=src)
+
+        def q_quant(b, G):
+            nc.vector.quantize_mx(out=qc[b][:, G, :].bitcast(FP8X4), scales=qs[b][:, G, :], in_=q_grp[b, G][:])
+
+        def kv_matmul(b, h, G, e4):
+            x = psum.tile([P, PACK, P], F32, name="bank")
+            c = slice(h * HALF + e4 * P, h * HALF + (e4 + 1) * P)
+            for t in range(PACK):
+                m = slice(G * HALF + t * P, G * HALF + (t + 1) * P)
+                for g in range(2):
+                    nc.tensor.matmul_mx(out=x[:, t, :], lhsT=kc[b][:, g, m].bitcast(FP8X4), lhsT_scale=ks[b][:, g, m],
+                                        rhs=vc[b][:, g, c].bitcast(FP8X4), rhs_scale=vs[b][:, g, c], start=(g == 0), stop=(g == 1))
+            acc[b, h, G, e4] = x
+
+        def kv_copy(b, h, G, e4, eng):
+            if e4 == 0:
+                m_grp[b, h, G] = work.tile([P, HALF * PACK], BF16, name="m_grp", align_bytes=64, bufs=5)
+            dst = m_grp[b, h, G][:, e4 * 512:(e4 + 1) * 512].rearrange("p (n t) -> p n t", t=PACK)
+            src = acc[b, h, G, e4][:].rearrange("p t n -> p n t")
+            if eng == "S":
+                nc.scalar.copy(out=dst, in_=src)
+            else:
+                nc.vector.tensor_copy(out=dst, in_=src)
+
+        def kv_quant(b, h, G):
+            c = slice(h * HALF, (h + 1) * HALF)
+            nc.vector.quantize_mx(out=mc[b][:, G, c].bitcast(FP8X4), scales=ms[b][:, G, c], in_=m_grp[b, h, G][:])
+
+        def out_matmul(b, h, r):
+            x = psum.tile([P, HALF], F32, name="bank")
+            m, c = slice(r * P, (r + 1) * P), slice(h * HALF, (h + 1) * HALF)
+            for G in range(2):
+                nc.tensor.matmul_mx(out=x[:], lhsT=qc[b][:, G, m].bitcast(FP8X4), lhsT_scale=qs[b][:, G, m],
+                                    rhs=mc[b][:, G, c].bitcast(FP8X4), rhs_scale=ms[b][:, G, c], start=(G == 0), stop=(G == 1))
+            acc[b, h, r] = x
+
+        def out_copy(b, h, r, eng):
+            t = work.tile([P, HALF], F32, name="res", bufs=6)
+            if eng == "S":
+                nc.scalar.activation(out=t[:], in_=acc[b, h, r][:], func=COPY, scale=INV)
+            else:
+                nc.vector.tensor_scalar(out=t[:], in0=acc[b, h, r][:], scalar1=INV, scalar2=None, op0=MULT)
+            nc.sync.dma_start(out=out[b].rearrange("(p r) e -> p r e", r=8)[:, r, h * HALF:(h + 1) * HALF], in_=t[:])
+
+        steps = (
+            "lv00 lk000 lv01 lq00 lq01 lk001 lk010  W000:V KI000 W010:S W001:S TR00 "
+            "TR01 VI000 W011:S lv10 lq10 lk011 lv11 lq11 KQ000 VQ000 QC00:S VI010 "
+            "VI001 QC01:S KI001 VQ001 lk100 lk101 lk110 KQ001 VI011 S1000 VQ010 W100:S "
+            "VQ011 KI010 lk111 KI011 KQ010 KC000:S S1010 KC010:S VI100 KQ011 VQ100 KI100 "
+            "MQ000 TR10 QC10:S KI101 TR11 W101:S KQ100 S1001 VI101 QC11:S KQ101 VQ101 "
+            "S1011 KC001:S KC011:S S1100 QQ00 KC100:S QQ01 MQ001 KI110 KI111 S2000 MQ011 "
+            "KQ110 KQ111 OC000:S S2001 W110:V MQ010 W111:V S1101 VI110 VI111 VQ110 OC001:S "
+            "VQ111 KC101:S QQ10 MQ101 S2010 S2011 OC010:S QQ11 MQ100 S1110 OC011:S KC110:V "
+            "S1111 S2100 KC111:A OC100:S S2101 MQ110 MQ111 OC101:A S2110 OC110:A S2111 OC111:A "
+        )
+        for item in steps.split(" "):
+            if item == "":
+                continue
+            name = item.split(":")[0]
+            eng = item.split(":")[1] if ":" in item else ""
+            op = name[0:2] if name[0] != "W" else "W"
+            a = [int(c) for c in name[len(op):]]
+            es = [eng] * 4 if eng != "A" else ["S", "V", "S", "V"]
+            if eng == "B":
+                es = ["V", "S", "V", "S"]
+            if op == "lk":
+                load_k(*a)
+            elif op == "lv":
+                load_v(*a)
+            elif op == "lq":
+                load_q(*a)
+            elif op == "KI":
+                k_interleave(*a)
+            elif op == "KQ":
+                k_quant(*a)
+            elif op == "W":
+                v_widen(*a, eng)
+            elif op == "VI":
+                v_interleave(*a)
+            elif op == "VQ":
+                v_quant(*a)
+            elif op == "QQ":
+                q_quant(*a)
+            elif op == "MQ":
+                kv_quant(*a)
+            elif op == "TR":
+                for i in range(4):
+                    q_transpose(a[0], a[1], i)
+            elif op == "QC":
+                for i in range(4):
+                    q_copy(a[0], a[1], i, es[i])
+            elif op == "S1":
+                for i in range(4):
+                    kv_matmul(a[0], a[1], a[2], i)
+            elif op == "KC":
+                for i in range(4):
+                    kv_copy(a[0], a[1], a[2], i, es[i])
+            elif op == "S2":
+                for i in range(4):
+                    out_matmul(a[0], a[1], 4 * a[2] + i)
+            elif op == "OC":
+                for i in range(4):
+                    out_copy(a[0], a[1], 4 * a[2] + i, es[i])

@@ -50,10 +50,10 @@ def tile_efficientattention_kernel(tc, q, k, v_bytes, v_scale, out):
         k_raw, v_raw, q_raw = {}, {}, {}
         v_wide, k_grp, v_grp, q_grp, m_grp, xt, acc, res = {}, {}, {}, {}, {}, {}, {}, {}
 
-        def load_k(b, G, g):
-            t = raw.tile([P, PACK, HALF], BF16, name="k_raw", bufs=5)
-            nc.sync.dma_start(out=t[:], in_=k[b].rearrange("(g p j) d -> g p j d", p=P, j=PACK)[g][:, :, G * HALF:(G + 1) * HALF])
-            k_raw[b, G, g] = t
+        def load_k(b, g):
+            t = raw.tile([P, PACK, D], BF16, name="k_raw", bufs=3)
+            nc.sync.dma_start(out=t[:], in_=k[b].rearrange("(g p j) d -> g p j d", p=P, j=PACK)[g])
+            k_raw[b, g] = t
 
         def load_v(b, g):
             t = raw.tile([P, PACK, E], U8, name="v_raw", bufs=2)
@@ -61,15 +61,15 @@ def tile_efficientattention_kernel(tc, q, k, v_bytes, v_scale, out):
             v_raw[b, g] = t
 
         def load_q(b, a):
-            t = raw.tile([P, 4, D], BF16, name="q_raw", bufs=4)
+            t = raw.tile([P, 4, D], BF16, name="q_raw", bufs=3)
             nc.sync.dma_start(out=t[:], in_=q[b].rearrange("(p r) d -> p r d", r=8)[:, 4 * a:4 * a + 4, :])
             q_raw[b, a] = t
 
         def k_interleave(b, G, g):
-            t = work.tile([P, HALF * PACK], BF16, name="k_grp", align_bytes=64, bufs=2)
+            t = work.tile([P, HALF * PACK], BF16, name="k_grp", align_bytes=64)
             nc.vector.tensor_scalar(
-                out=t[:].rearrange("p (t m j) -> p t m j", t=PACK, j=PACK),
-                in0=k_raw[b, G, g][:].rearrange("p j (m t) -> p t m j", t=PACK),
+                out=t[:].rearrange("p (t m j) -> p m j t", t=PACK, j=PACK),
+                in0=k_raw[b, g][:, :, G * HALF:(G + 1) * HALF].rearrange("p j (m t) -> p m j t", t=PACK),
                 scalar1=INV, scalar2=None, op0=MULT)
             k_grp[b, G, g] = t
 
@@ -89,7 +89,7 @@ def tile_efficientattention_kernel(tc, q, k, v_bytes, v_scale, out):
 
         def v_interleave(b, h, g):
             t = work.tile([P, HALF * PACK], BF16, name="v_grp", align_bytes=64)
-            nc.vector.tensor_copy(out=t[:].rearrange("p (e j) -> p e j", j=PACK), in_=v_wide[b, h, g][:].rearrange("p j e -> p e j"))
+            nc.vector.tensor_copy(out=t[:].rearrange("p (c i j) -> p c j i", i=4, j=PACK), in_=v_wide[b, h, g][:].rearrange("p j (c i) -> p c j i", i=4))
             v_grp[b, h, g] = t
 
         def v_quant(b, h, g):
@@ -159,15 +159,15 @@ def tile_efficientattention_kernel(tc, q, k, v_bytes, v_scale, out):
             nc.sync.dma_start(out=out[b].rearrange("(p r) e -> p r e", r=8)[:, r, h * HALF:(h + 1) * HALF], in_=t[:])
 
         steps = (
-            "lv00 lk000 lv01 lq00 lq01 lk001 lk010  W000:V KI000 W010:S W001:S TR00 "
-            "TR01 VI000 W011:S lv10 lq10 lk011 lv11 lq11 KQ000 VQ000 QC00:S VI010 "
-            "VI001 QC01:S KI001 VQ001 lk100 lk101 lk110 KQ001 VI011 S1000 VQ010 W100:S "
-            "VQ011 KI010 lk111 KI011 KQ010 KC000:S S1010 KC010:S VI100 KQ011 VQ100 KI100 "
-            "MQ000 TR10 QC10:S KI101 TR11 W101:S KQ100 S1001 VI101 QC11:S KQ101 VQ101 "
-            "S1011 KC001:S KC011:S S1100 QQ00 KC100:S QQ01 MQ001 KI110 KI111 S2000 MQ011 "
-            "KQ110 KQ111 OC000:S S2001 W110:V MQ010 W111:V S1101 VI110 VI111 VQ110 OC001:S "
-            "VQ111 KC101:S QQ10 MQ101 S2010 S2011 OC010:S QQ11 MQ100 S1110 OC011:S KC110:V "
-            "S1111 S2100 KC111:A OC100:S S2101 MQ110 MQ111 OC101:A S2110 OC110:A S2111 OC111:A "
+            "lv00 lv01 lk00 lq00 lq01 lk01 TR00 W000:V W010:S TR01 lv10 lq10 "
+            "lq11 lk10 W001:S VI000 VI010 W011:S lv11 QC00:S KI000 VQ010 VQ000 VI001 "
+            "KQ000 VI011 QC01:S KI001 W100:S VQ001 KQ001 S1000 VQ011 KI011 S1010 KC000:S "
+            "TR10 KI010 lk11 W110:V VI100 KQ011 KC010:S QC10:S KQ010 KI100 W101:S S1011 "
+            "VQ100 KQ100 KI101 QQ00 VI101 KC011:S KQ101 S1001 TR11 VQ101 MQ011 KC001:S "
+            "QQ01 MQ010 KI110 KI111 S1100 KQ110 KQ111 MQ001 QC11:S MQ000 KC100:S W111:V "
+            "S2010 OC010:S S2011 VI110 VI111 VQ110 VQ111 OC011:S QQ10 S1101 KC101:S S2000 "
+            "OC000:S QQ11 MQ100 MQ101 S2001 OC001:S S1111 S2100 KC111:A S1110 OC100:S S2101 "
+            "OC101:S KC110:V MQ111 MQ110 S2110 S2111 OC110:S OC111:A "
         )
         for item in steps.split(" "):
             if item == "":

from contextlib import ExitStack

import concourse.mybir as mybir
from concourse.masks import make_identity

B, S, D, E = 2, 1024, 1024, 1024
FLOPS = 2 * B * (D * S * E + S * D * E)

F32 = mybir.dt.float32
BF16 = mybir.dt.bfloat16
U32 = mybir.dt.uint32
U8 = mybir.dt.uint8
FP8 = mybir.dt.float8_e4m3fn
FP8X4 = mybir.dt.float8_e4m3fn_x4
COPY = mybir.ActivationFunctionType.Copy
MULT = mybir.AluOpType.mult

P = 128
PACK = 4
HALF = 512
INV = 1.0 / 32.0


def tile_efficientattention_kernel(tc, q, k, v_bytes, v_scale, out):
    nc = tc.nc
    with ExitStack() as ctx:
        keep = ctx.enter_context(tc.tile_pool(name="keep", bufs=1))
        raw = ctx.enter_context(tc.tile_pool(name="raw", bufs=4))
        work = ctx.enter_context(tc.tile_pool(name="work", bufs=3))
        psum = ctx.enter_context(tc.psum_pool(name="psum", bufs=8))
        ctx.enter_context(tc.manual_schedule())

        scl = keep.tile([P, 2, PACK], F32, name="scl")
        nc.scalar.dma_start(out=scl[:], in_=v_scale.rearrange("o (g p j) x -> p (o g) (j x)", p=P, j=PACK))
        ident = keep.tile([P, P], F32, name="ident")
        make_identity(nc, ident[:])
        warm = keep.tile([P, 1], F32, name="warm")
        nc.vector.memset(warm[:], 0.0)
        nc.scalar.activation(out=warm[:], in_=warm[:], func=COPY, scale=1.0)

        kc = [keep.tile([P, 2, D], U32, name=f"kc{b}", align_bytes=64) for b in range(B)]
        ks = [keep.tile([P, 2, D], U8, name=f"ks{b}", align_bytes=64) for b in range(B)]
        vc = [keep.tile([P, 2, E], U32, name=f"vc{b}", align_bytes=64) for b in range(B)]
        vs = [keep.tile([P, 2, E], U8, name=f"vs{b}", align_bytes=64) for b in range(B)]
        qc = [keep.tile([P, 2, S], U32, name=f"qc{b}", align_bytes=64) for b in range(B)]
        qs = [keep.tile([P, 2, S], U8, name=f"qs{b}", align_bytes=64) for b in range(B)]
        mc = [keep.tile([P, 2, E], U32, name=f"mc{b}", align_bytes=64) for b in range(B)]
        ms = [keep.tile([P, 2, E], U8, name=f"ms{b}", align_bytes=64) for b in range(B)]

        k_raw, v_raw, q_raw = {}, {}, {}
        v_wide, k_grp, v_grp, q_grp, m_grp, xt, acc, res = {}, {}, {}, {}, {}, {}, {}, {}

        def load_k(b, g):
            t = raw.tile([P, PACK, D], BF16, name="k_raw", bufs=3)
            nc.sync.dma_start(out=t[:], in_=k[b].rearrange("(g p j) d -> g p j d", p=P, j=PACK)[g])
            k_raw[b, g] = t

        def load_v(b, g):
            t = raw.tile([P, PACK, E], U8, name="v_raw", bufs=2)
            nc.sync.dma_start(out=t[:], in_=v_bytes[b].rearrange("(g p j) e -> g p j e", p=P, j=PACK)[g])
            v_raw[b, g] = t

        def load_q(b, a):
            t = raw.tile([P, 4, D], BF16, name="q_raw", bufs=3)
            nc.sync.dma_start(out=t[:], in_=q[b].rearrange("(p r) d -> p r d", r=8)[:, 4 * a:4 * a + 4, :])
            q_raw[b, a] = t

        def k_interleave(b, G, g):
            t = work.tile([P, HALF * PACK], BF16, name="k_grp", align_bytes=64)
            nc.vector.tensor_scalar(
                out=t[:].rearrange("p (t m j) -> p m j t", t=PACK, j=PACK),
                in0=k_raw[b, g][:, :, G * HALF:(G + 1) * HALF].rearrange("p j (m t) -> p m j t", t=PACK),
                scalar1=INV, scalar2=None, op0=MULT)
            k_grp[b, G, g] = t

        def k_quant(b, G, g):
            c = slice(G * HALF, (G + 1) * HALF)
            nc.vector.quantize_mx(out=kc[b][:, g, c].bitcast(FP8X4), scales=ks[b][:, g, c], in_=k_grp[b, G, g][:])

        def v_widen(b, h, g, eng):
            t = work.tile([P, PACK, HALF], BF16, name="v_wide", bufs=3)
            for j in range(PACK):
                src = v_raw[b, g][:, j, h * HALF:(h + 1) * HALF].bitcast(FP8)
                if eng == "S":
                    nc.scalar.activation(out=t[:, j, :], in_=src, func=COPY, scale=scl[:, g, j:j + 1])
                else:
                    nc.vector.tensor_scalar(out=t[:, j, :], in0=src, scalar1=scl[:, g, j:j + 1], scalar2=None, op0=MULT)
            v_wide[b, h, g] = t

        def v_interleave(b, h, g):
            t = work.tile([P, HALF * PACK], BF16, name="v_grp", align_bytes=64)
            nc.vector.tensor_copy(out=t[:].rearrange("p (c i j) -> p c j i", i=4, j=PACK), in_=v_wide[b, h, g][:].rearrange("p j (c i) -> p c j i", i=4))
            v_grp[b, h, g] = t

        def v_quant(b, h, g):
            c = slice(h * HALF, (h + 1) * HALF)
            nc.vector.quantize_mx(out=vc[b][:, g, c].bitcast(FP8X4), scales=vs[b][:, g, c], in_=v_grp[b, h, g][:])

        def q_transpose(b, G, i):
            x = psum.tile([P, 2, 2, P], F32, name="bank")
            for r in range(2):
                row = 2 * i + r
                words = q_raw[b, row // 4][:, row % 4, :].bitcast(F32)
                for u in range(2):
                    nc.tensor.transpose(x[:, r, u, :], words[:, 256 * G + u:256 * (G + 1):2], ident[:])
            xt[b, G, i] = x

        def q_copy(b, G, i, eng):
            if i == 0:
                q_grp[b, G] = work.tile([P, S * PACK], BF16, name="q_grp", align_bytes=64, bufs=4)
            dst = q_grp[b, G][:, i * 1024:(i + 1) * 1024].bitcast(F32).rearrange("p (r n u) -> p r n u", r=2, u=2)
            src = xt[b, G, i][:].rearrange("p r u n -> p r n u")
            if eng == "S":
                nc.scalar.copy(out=dst, in_=src)
            else:
                nc.vector.tensor_copy(out=dst, in_=src)

        def q_quant(b, G):
            nc.vector.quantize_mx(out=qc[b][:, G, :].bitcast(FP8X4), scales=qs[b][:, G, :], in_=q_grp[b, G][:])

        def kv_matmul(b, h, G, e4):
            x = psum.tile([P, PACK, P], F32, name="bank")
            c = slice(h * HALF + e4 * P, h * HALF + (e4 + 1) * P)
            for t in range(PACK):
                m = slice(G * HALF + t * P, G * HALF + (t + 1) * P)
                for g in range(2):
                    nc.tensor.matmul_mx(out=x[:, t, :], lhsT=kc[b][:, g, m].bitcast(FP8X4), lhsT_scale=ks[b][:, g, m],
                                        rhs=vc[b][:, g, c].bitcast(FP8X4), rhs_scale=vs[b][:, g, c], start=(g == 0), stop=(g == 1))
            acc[b, h, G, e4] = x

        def kv_copy(b, h, G, e4, eng):
            if e4 == 0:
                m_grp[b, h, G] = work.tile([P, HALF * PACK], BF16, name="m_grp", align_bytes=64, bufs=5)
            dst = m_grp[b, h, G][:, e4 * 512:(e4 + 1) * 512].rearrange("p (n t) -> p n t", t=PACK)
            src = acc[b, h, G, e4][:].rearrange("p t n -> p n t")
            if eng == "S":
                nc.scalar.copy(out=dst, in_=src)
            else:
                nc.vector.tensor_copy(out=dst, in_=src)

        def kv_quant(b, h, G):
            c = slice(h * HALF, (h + 1) * HALF)
            nc.vector.quantize_mx(out=mc[b][:, G, c].bitcast(FP8X4), scales=ms[b][:, G, c], in_=m_grp[b, h, G][:])

        def out_matmul(b, h, r):
            x = psum.tile([P, HALF], F32, name="bank")
            m, c = slice(r * P, (r + 1) * P), slice(h * HALF, (h + 1) * HALF)
            for G in range(2):
                nc.tensor.matmul_mx(out=x[:], lhsT=qc[b][:, G, m].bitcast(FP8X4), lhsT_scale=qs[b][:, G, m],
                                    rhs=mc[b][:, G, c].bitcast(FP8X4), rhs_scale=ms[b][:, G, c], start=(G == 0), stop=(G == 1))
            acc[b, h, r] = x

        def out_copy(b, h, r, eng):
            t = work.tile([P, HALF], F32, name="res", bufs=6)
            if eng == "S":
                nc.scalar.activation(out=t[:], in_=acc[b, h, r][:], func=COPY, scale=INV)
            else:
                nc.vector.tensor_scalar(out=t[:], in0=acc[b, h, r][:], scalar1=INV, scalar2=None, op0=MULT)
            nc.sync.dma_start(out=out[b].rearrange("(p r) e -> p r e", r=8)[:, r, h * HALF:(h + 1) * HALF], in_=t[:])

        steps = (
            "lv00 lv01 lk00 lq00 lq01 lk01 TR00 W000:V W010:S TR01 lv10 lq10 "
            "lq11 lk10 W001:S VI000 VI010 W011:S lv11 QC00:S KI000 VQ010 VQ000 VI001 "
            "KQ000 VI011 QC01:S KI001 W100:S VQ001 KQ001 S1000 VQ011 KI011 S1010 KC000:S "
            "TR10 KI010 lk11 W110:V VI100 KQ011 KC010:S QC10:S KQ010 KI100 W101:S S1011 "
            "VQ100 KQ100 KI101 QQ00 VI101 KC011:S KQ101 S1001 TR11 VQ101 MQ011 KC001:S "
            "QQ01 MQ010 KI110 KI111 S1100 KQ110 KQ111 MQ001 QC11:S MQ000 KC100:S W111:V "
            "S2010 OC010:S S2011 VI110 VI111 VQ110 VQ111 OC011:S QQ10 S1101 KC101:S S2000 "
            "OC000:S QQ11 MQ100 MQ101 S2001 OC001:S S1111 S2100 KC111:A S1110 OC100:S S2101 "
            "OC101:S KC110:V MQ111 MQ110 S2110 S2111 OC110:S OC111:A "
        )
        for item in steps.split(" "):
            if item == "":
                continue
            name = item.split(":")[0]
            eng = item.split(":")[1] if ":" in item else ""
            op = name[0:2] if name[0] != "W" else "W"
            a = [int(c) for c in name[len(op):]]
            es = [eng] * 4 if eng != "A" else ["S", "V", "S", "V"]
            if eng == "B":
                es = ["V", "S", "V", "S"]
            if op == "lk":
                load_k(*a)
            elif op == "lv":
                load_v(*a)
            elif op == "lq":
                load_q(*a)
            elif op == "KI":
                k_interleave(*a)
            elif op == "KQ":
                k_quant(*a)
            elif op == "W":
                v_widen(*a, eng)
            elif op == "VI":
                v_interleave(*a)
            elif op == "VQ":
                v_quant(*a)
            elif op == "QQ":
                q_quant(*a)
            elif op == "MQ":
                kv_quant(*a)
            elif op == "TR":
                for i in range(4):
                    q_transpose(a[0], a[1], i)
            elif op == "QC":
                for i in range(4):
                    q_copy(a[0], a[1], i, es[i])
            elif op == "S1":
                for i in range(4):
                    kv_matmul(a[0], a[1], a[2], i)
            elif op == "KC":
                for i in range(4):
                    kv_copy(a[0], a[1], a[2], i, es[i])
            elif op == "S2":
                for i in range(4):
                    out_matmul(a[0], a[1], 4 * a[2] + i)
            elif op == "OC":
                for i in range(4):
                    out_copy(a[0], a[1], 4 * a[2] + i, es[i])
